import numpy as np
import ml_dtypes


def mxq(x, axis, fmt="e4m3"):
    dtype, down = {"e4m3": (ml_dtypes.float8_e4m3fn, 7), "e5m2": (ml_dtypes.float8_e5m2, 14)}[fmt]
    v = np.moveaxis(np.asarray(x, np.float32).astype(ml_dtypes.bfloat16).astype(np.float64), axis, -1)
    blocks = v.reshape(v.shape[:-1] + (-1, 32))
    amax = np.abs(blocks).max(-1, keepdims=True)
    byte = np.maximum(np.where(amax > 0, np.frexp(amax)[1] - 1 + 127, 0) - down, 1)
    scale = np.exp2(byte - 127.0)
    codes = (blocks / scale).astype(np.float32).astype(dtype).astype(np.float64)
    return np.moveaxis((codes * scale).reshape(v.shape), -1, axis)


WIDE = False


def mx_kscale(k):
    if not WIDE:
        return np.ones(k)
    levels = np.array([18, -18])
    if k % 512:
        return np.exp2(np.random.permutation(np.resize(levels, k // 32))).repeat(32)
    a = np.empty((k // 512, 16))
    for p in range(k // 512):
        a[p, :8] = np.random.permutation(np.resize(levels, 8))
        for g in range(8):
            far = levels[np.abs(levels - a[p, g]) >= 10]
            a[p, g + 8] = far[np.random.randint(len(far))]
    return np.exp2(a.ravel()).repeat(32)


BF16 = ml_dtypes.bfloat16


def bf(x):
    return np.asarray(x, np.float32).astype(BF16)


def f64(x):
    return np.asarray(x).astype(np.float64)


B, S, D = 8, 512, 512


def decay_of(gamma):
    pos = np.arange(S)
    diff = pos[:, None] - pos[None, :]
    causal = diff >= 0
    return np.where(causal, f64(gamma)[0] ** np.where(causal, diff, 0), 0.0)


def setup_inputs():
    u = mx_kscale(D)
    c = mx_kscale(S)
    s = mx_kscale(S)
    a = D ** -0.25
    q0 = bf(np.random.standard_normal((B, S, D)) * a)
    k0 = bf(np.random.standard_normal((B, S, D)) * a)
    v0 = bf(np.random.standard_normal((B, S, D)) * 0.5)
    gamma = bf(1.0 - 0.00390625 * np.random.randint(1, 3, (1,)))
    g = bf(np.random.standard_normal((B, S, D)) * np.exp2(np.random.randint(-6, 1, (B, S, 1))) / s[:, None] * u)
    decay = decay_of(gamma)
    return {"q_rot": bf(f64(q0) * s[:, None]), "k_rot": bf(f64(k0) / c[:, None]), "v": bf(f64(v0) * c[:, None] / u),
            "gamma": gamma, "decay": np.asarray(decay, np.float32), "grad_out": g}


def reference(q_rot, k_rot, v, gamma, decay, grad_out):
    dp = mxq(f64(grad_out), 2, "e5m2") @ mxq(f64(v), 2, "e4m3").transpose(0, 2, 1)
    dz1 = dp * f64(decay)[None]
    dq = mxq(dz1, 2, "e5m2") @ mxq(f64(k_rot), 1, "e4m3")
    dk = mxq(dz1, 1, "e5m2").transpose(0, 2, 1) @ mxq(f64(q_rot), 1, "e4m3")
    return dq, dk

@@ -1,0 +1,236 @@
+from contextlib import ExitStack
+
+import concourse.mybir as mybir
+from concourse.masks import make_identity
+
+B, S, D = 8, 512, 512
+FLOPS = 3 * 2 * B * S * S * D
+
+F32 = mybir.dt.float32
+BF16 = mybir.dt.bfloat16
+U32 = mybir.dt.uint32
+U8 = mybir.dt.uint8
+E4M3 = mybir.dt.float8_e4m3fn_x4
+E5M2 = mybir.dt.float8_e5m2_x4
+
+P = 128
+AHEAD = 3
+K_SHARE = 256
+
+
+def tile_retention_pa_v_kernel(tc, q_rot, k_rot, v, gamma, decay, grad_out, out_0, out_1):
+    nc = tc.nc
+    mult = mybir.AluOpType.mult
+
+    with ExitStack() as ctx:
+        const = ctx.enter_context(tc.tile_pool(name="const", bufs=1))
+        loads = ctx.enter_context(tc.tile_pool(name="loads", bufs=AHEAD + 1))
+        work = ctx.enter_context(tc.tile_pool(name="work", bufs=2))
+        results = ctx.enter_context(tc.tile_pool(name="results", bufs=8))
+        ps_tr = ctx.enter_context(tc.psum_pool(name="ps_tr", bufs=2))
+        ps_dp = ctx.enter_context(tc.psum_pool(name="ps_dp", bufs=2))
+        ps_out = ctx.enter_context(tc.psum_pool(name="ps_out", bufs=4))
+
+        ident = const.tile([P, P], F32)
+        make_identity(nc, ident[:])
+        dec_nat = const.tile([P, 4, S], F32)
+        dec = const.tile([P, 4, S], F32)
+
+        ctx.enter_context(tc.manual_schedule())
+
+        raw = {}
+        grp = {}
+        codes = {}
+        dz = {}
+        res = {}
+
+        def rows4(x):
+            return x.rearrange("(p j) d -> p j d", j=4)
+
+        def load(name, x, b, pieces=1):
+            t = loads.tile([P, 4, D], BF16, name="raw_" + name)
+            w = 4 // pieces
+            for h in range(pieces):
+                nc.sync.dma_start(out=t[:, h * w : (h + 1) * w, :], in_=rows4(x[b])[:, h * w : (h + 1) * w, :])
+            raw[name, b] = t
+
+        def load_seq(b):
+            load("g", grad_out, b)
+            load("v", v, b)
+            load("q", q_rot, b)
+            load("k", k_rot, b)
+
+        def grouped(name, b, width=S):
+            t = work.tile([P, width, 4], BF16, name="grp_" + name, align_bytes=64)
+            grp[name, b] = t
+
+        def quantise(name, b, fmt, width=S):
+            c = work.tile([P, width], U32, name="codes_" + name, align_bytes=64)
+            s = work.tile([P, width], U8, name="scales_" + name, align_bytes=64)
+            nc.vector.quantize_mx(
+                out=c[:].bitcast(fmt), scales=s[:], in_=grp[name, b][:].rearrange("p w t -> p (w t)")
+            )
+            codes[name, b] = (c, s)
+
+        def turn_bank(words_of, name, b, h, order, copy):
+            ps = ps_tr.tile([P, 2, 2, P], F32, name="tr")
+            for j in range(2):
+                for u in range(2):
+                    nc.tensor.transpose(ps[:, j, u, :], words_of(2 * h + j, u), ident[:])
+            words = grp[name, b][:].rearrange("p w t -> p (w t)").bitcast(F32)[:, 512 * h : 512 * (h + 1)]
+            if order == "jr":
+                copy(out=words.rearrange("p (j r u) -> p j r u", j=2, u=2), in_=ps[:].rearrange("p j u r -> p j r u"))
+            else:
+                copy(out=words.rearrange("p (r j u) -> p r j u", j=2, u=2), in_=ps[:].rearrange("p j u r -> p r j u"))
+
+        def turn_g(b, h, copy):
+            w = raw["g", b][:].bitcast(F32)
+            turn_bank(lambda j, u: w[:, j, u : 256 : 2], "g", b, h, "jr", copy)
+
+        def turn_v(b, h, copy):
+            w = raw["v", b][:].bitcast(F32)
+            turn_bank(lambda j, u: w[:, j, u : 256 : 2], "v", b, h, "rj", copy)
+
+        def turn_a(b, h, copy):
+            w = dz[b][:].bitcast(F32)
+            turn_bank(lambda j, u: w[:, j, 128 * u : 128 * (u + 1)], "a", b, h, "jr", copy)
+
+        def mm(ps, lhs, rhs, j, rhs0=0):
+            lc, ls = lhs
+            rc, rs = rhs
+            cols = slice(P * j, P * (j + 1))
+            rcols = slice(rhs0, rhs0 + 512)
+            nc.tensor.matmul_mx(
+                out=ps[:],
+                lhsT=lc[:, cols].bitcast(E5M2),
+                lhsT_scale=ls[:, cols],
+                rhs=rc[:, rcols].bitcast(E4M3),
+                rhs_scale=rs[:, rcols],
+                start=True,
+                stop=True,
+            )
+
+        dps = {}
+
+        def dp(b, t):
+            ps = ps_dp.tile([P, S], F32, name="dp")
+            mm(ps, codes["g", b], codes["v", b], t)
+            dps[b, t] = ps
+
+        def times_decay(b, t):
+            if t == 0:
+                dz_t = work.tile([P, 4, S], BF16, name="dz")
+                dz[b] = dz_t
+            nc.vector.tensor_tensor(out=dz[b][:, t, :], in0=dps[b, t][:], in1=dec[:, t, :], op=mult)
+
+        def interleave(copy, dst, src):
+            copy(out=dst.rearrange("p (c i) t -> p c t i", i=4), in_=src.rearrange("p t (c i) -> p c t i", i=4))
+
+        def group_b(b):
+            grouped("b", b)
+            pairs = dz[b][:].rearrange("p t (u r e) -> p t u r e", u=2, e=2)
+            for j in range(4):
+                interleave(
+                    nc.vector.tensor_copy, grp["b", b][:, P * j : P * (j + 1), :], pairs[:, :, j // 2, :, j % 2]
+                )
+
+        def group_qk(which, b, lo, hi, copy):
+            o = 0 if which == "q" else D
+            interleave(copy, grp["qk", b][:, o + lo : o + hi, :], raw[which, b][:, :, lo:hi])
+
+        def product(which, b, t, copy, per_store=2):
+            ps = ps_out.tile([P, D], F32, name="po")
+            if which == "dq":
+                mm(ps, codes["a", b], codes["qk", b], t, D)
+                dst = out_0
+            else:
+                mm(ps, codes["b", b], codes["qk", b], t, 0)
+                dst = out_1
+            if t % per_store == 0:
+                r = results.tile([P, 2, D], F32, name="res")
+                res[0] = r
+            copy(out=res[0][:, t % per_store, :], in_=ps[:])
+            if t % per_store == per_store - 1:
+                t0 = t + 1 - per_store
+                nc.sync.dma_start(out=rows4(dst[b])[:, t0 : t + 1, :], in_=res[0][:, 0:per_store, :])
+
+        scopy = nc.scalar.copy
+        vcopy = nc.vector.tensor_copy
+
+        load("g", grad_out, 0, 2)
+        load("v", v, 0, 2)
+        for t in range(4):
+            nc.sync.dma_start(out=dec_nat[:, t, :], in_=rows4(decay)[:, t, :])
+        load("q", q_rot, 0)
+        load("k", k_rot, 0)
+        for b in range(1, AHEAD):
+            load_seq(b)
+        grouped("g", 0)
+        grouped("v", 0)
+        turn_g(0, 0, scopy)
+        turn_g(0, 1, vcopy)
+        turn_v(0, 0, scopy)
+        quantise("g", 0, E5M2)
+        turn_v(0, 1, scopy)
+        for t in range(4):
+            (vcopy if t == 0 else scopy)(
+                out=dec[:, t, :].rearrange("p (u r e) -> p u r e", u=2, e=2),
+                in_=dec_nat[:, t, :].rearrange("p (r u e) -> p u r e", u=2, e=2),
+            )
+            if t == 0:
+                quantise("v", 0, E4M3)
+
+        for i in range(B):
+            n = i + 1
+            more = n < B
+            if i + AHEAD < B:
+                load_seq(i + AHEAD)
+            dp(i, 0)
+            dp(i, 1)
+            if more:
+                grouped("g", n)
+                turn_g(n, 0, scopy)
+                turn_g(n, 1, scopy)
+            times_decay(i, 0)
+            times_decay(i, 1)
+            dp(i, 2)
+            dp(i, 3)
+            times_decay(i, 2)
+            times_decay(i, 3)
+            if i == 0:
+                grouped("qk", 0, 2 * D)
+                group_qk("q", 0, 0, D, vcopy)
+                group_qk("k", 0, 0, D, scopy)
+            if more:
+                quantise("g", n, E5M2)
+            if i > 0:
+                product("dq", i - 1, 0, scopy)
+                product("dq", i - 1, 1, scopy)
+            if more:
+                grouped("v", n)
+                turn_v(n, 0, scopy)
+                turn_v(n, 1, scopy)
+            grouped("a", i)
+            turn_a(i, 0, scopy)
+            turn_a(i, 1, scopy)
+            group_b(i)
+            if i == 0:
+                quantise("qk", 0, E4M3, 2 * D)
+            if more:
+                quantise("v", n, E4M3)
+            if i > 0:
+                product("dq", i - 1, 2, scopy)
+                product("dq", i - 1, 3, scopy)
+            quantise("b", i, E5M2)
+            if more:
+                grouped("qk", n, 2 * D)
+                group_qk("k", n, 0, K_SHARE, scopy)
+                group_qk("q", n, 0, D, vcopy)
+                group_qk("k", n, K_SHARE, D, vcopy)
+            quantise("a", i, E5M2)
+            if more:
+                quantise("qk", n, E4M3, 2 * D)
+            for t in range(4):
+                product("dk", i, t, scopy if more or t % 2 == 0 else vcopy)
+        for t in range(4):
+            product("dq", B - 1, t, scopy if t % 2 == 0 else vcopy, 1)

@@ -15,7 +15,7 @@ E5M2 = mybir.dt.float8_e5m2_x4
 
 P = 128
 AHEAD = 3
-K_SHARE = 256
+K_SHARE = 320
 
 
 def tile_retention_pa_v_kernel(tc, q_rot, k_rot, v, gamma, decay, grad_out, out_0, out_1):
@@ -72,28 +72,26 @@ def tile_retention_pa_v_kernel(tc, q_rot, k_rot, v, gamma, decay, grad_out, out_
             )
             codes[name, b] = (c, s)
 
-        def turn_bank(words_of, name, b, h, order, copy):
+        banks = {}
+
+        def turn(name, b, h):
+            src = dz[b] if name == "a" else raw[name, b]
+            words = src[:].bitcast(F32)
             ps = ps_tr.tile([P, 2, 2, P], F32, name="tr")
             for j in range(2):
                 for u in range(2):
-                    nc.tensor.transpose(ps[:, j, u, :], words_of(2 * h + j, u), ident[:])
+                    cols = slice(P * u, P * (u + 1)) if name == "a" else slice(u, 2 * P, 2)
+                    nc.tensor.transpose(ps[:, j, u, :], words[:, 2 * h + j, cols], ident[:])
+            banks[name, b, h] = ps
+
+        def untangle(name, b, h, copy):
+            ps = banks[name, b, h]
+            order = "rj" if name == "v" else "jr"
             words = grp[name, b][:].rearrange("p w t -> p (w t)").bitcast(F32)[:, 512 * h : 512 * (h + 1)]
             if order == "jr":
                 copy(out=words.rearrange("p (j r u) -> p j r u", j=2, u=2), in_=ps[:].rearrange("p j u r -> p j r u"))
             else:
                 copy(out=words.rearrange("p (r j u) -> p r j u", j=2, u=2), in_=ps[:].rearrange("p j u r -> p r j u"))
-
-        def turn_g(b, h, copy):
-            w = raw["g", b][:].bitcast(F32)
-            turn_bank(lambda j, u: w[:, j, u : 256 : 2], "g", b, h, "jr", copy)
-
-        def turn_v(b, h, copy):
-            w = raw["v", b][:].bitcast(F32)
-            turn_bank(lambda j, u: w[:, j, u : 256 : 2], "v", b, h, "rj", copy)
-
-        def turn_a(b, h, copy):
-            w = dz[b][:].bitcast(F32)
-            turn_bank(lambda j, u: w[:, j, 128 * u : 128 * (u + 1)], "a", b, h, "jr", copy)
 
         def mm(ps, lhs, rhs, j, rhs0=0):
             lc, ls = lhs
@@ -138,99 +136,143 @@ def tile_retention_pa_v_kernel(tc, q_rot, k_rot, v, gamma, decay, grad_out, out_
             o = 0 if which == "q" else D
             interleave(copy, grp["qk", b][:, o + lo : o + hi, :], raw[which, b][:, :, lo:hi])
 
-        def product(which, b, t, copy, per_store=2):
+        outs = {}
+
+        def product(which, b, t):
             ps = ps_out.tile([P, D], F32, name="po")
             if which == "dq":
                 mm(ps, codes["a", b], codes["qk", b], t, D)
-                dst = out_0
             else:
                 mm(ps, codes["b", b], codes["qk", b], t, 0)
-                dst = out_1
+            outs[which, b, t] = ps
+
+        def finish(which, b, t, copy, per_store=2):
+            dst = out_0 if which == "dq" else out_1
             if t % per_store == 0:
                 r = results.tile([P, 2, D], F32, name="res")
-                res[0] = r
-            copy(out=res[0][:, t % per_store, :], in_=ps[:])
+                res[which] = r
+            copy(out=res[which][:, t % per_store, :], in_=outs[which, b, t][:])
             if t % per_store == per_store - 1:
                 t0 = t + 1 - per_store
-                nc.sync.dma_start(out=rows4(dst[b])[:, t0 : t + 1, :], in_=res[0][:, 0:per_store, :])
+                nc.sync.dma_start(out=rows4(dst[b])[:, t0 : t + 1, :], in_=res[which][:, 0:per_store, :])
 
         scopy = nc.scalar.copy
         vcopy = nc.vector.tensor_copy
 
+        load("q", q_rot, 0)
         load("g", grad_out, 0, 2)
+        load("k", k_rot, 0)
         load("v", v, 0, 2)
         for t in range(4):
             nc.sync.dma_start(out=dec_nat[:, t, :], in_=rows4(decay)[:, t, :])
-        load("q", q_rot, 0)
-        load("k", k_rot, 0)
         for b in range(1, AHEAD):
             load_seq(b)
+        grouped("qk", 0, 2 * D)
         grouped("g", 0)
         grouped("v", 0)
-        turn_g(0, 0, scopy)
-        turn_g(0, 1, vcopy)
-        turn_v(0, 0, scopy)
+        for w in range(4):
+            ps = ps_out.tile([P, D], F32, name="po")
+            nc.tensor.matmul(ps[:], lhsT=raw["q", 0][:, w % 4, 0:P], rhs=raw["q", 0][:, w % 4, :], start=True, stop=True)
+        group_qk("q", 0, 0, 352, vcopy)
+        group_qk("q", 0, 352, D, scopy)
+        turn("g", 0, 0)
+        turn("g", 0, 1)
+        untangle("g", 0, 0, scopy)
+        untangle("g", 0, 1, vcopy)
+        group_qk("k", 0, 0, 384, vcopy)
+        group_qk("k", 0, 384, D, scopy)
+        for w in range(2):
+            ps = ps_out.tile([P, D], F32, name="po")
+            nc.tensor.matmul(ps[:], lhsT=raw["k", 0][:, w % 4, 0:P], rhs=raw["k", 0][:, w % 4, :], start=True, stop=True)
         quantise("g", 0, E5M2)
-        turn_v(0, 1, scopy)
+        turn("v", 0, 0)
+        turn("v", 0, 1)
+        untangle("v", 0, 0, scopy)
+        untangle("v", 0, 1, scopy)
         for t in range(4):
-            (vcopy if t == 0 else scopy)(
+            (vcopy if t < 1 else scopy)(
                 out=dec[:, t, :].rearrange("p (u r e) -> p u r e", u=2, e=2),
                 in_=dec_nat[:, t, :].rearrange("p (r u e) -> p u r e", u=2, e=2),
             )
             if t == 0:
                 quantise("v", 0, E4M3)
+                quantise("qk", 0, E4M3, 2 * D)
+                dp(0, 0)
+                dp(0, 1)
 
         for i in range(B):
             n = i + 1
             more = n < B
             if i + AHEAD < B:
                 load_seq(i + AHEAD)
-            dp(i, 0)
-            dp(i, 1)
-            if more:
+            if i == 0:
                 grouped("g", n)
-                turn_g(n, 0, scopy)
-                turn_g(n, 1, scopy)
+                turn("g", n, 0)
+                turn("g", n, 1)
             times_decay(i, 0)
             times_decay(i, 1)
             dp(i, 2)
             dp(i, 3)
             times_decay(i, 2)
             times_decay(i, 3)
-            if i == 0:
-                grouped("qk", 0, 2 * D)
-                group_qk("q", 0, 0, D, vcopy)
-                group_qk("k", 0, 0, D, scopy)
             if more:
+                if i == 0:
+                    group_b(0)
+                untangle("g", n, 0, scopy)
+                untangle("g", n, 1, scopy)
                 quantise("g", n, E5M2)
             if i > 0:
-                product("dq", i - 1, 0, scopy)
-                product("dq", i - 1, 1, scopy)
+                finish("dq", i - 1, 0, scopy)
+                finish("dq", i - 1, 1, scopy)
             if more:
                 grouped("v", n)
-                turn_v(n, 0, scopy)
-                turn_v(n, 1, scopy)
+                grouped("qk", n, 2 * D)
+                turn("v", n, 0)
+                turn("v", n, 1)
+                untangle("v", n, 0, scopy)
+                untangle("v", n, 1, scopy)
+            if i > 0:
+                product("dq", i - 1, 2)
+                product("dq", i - 1, 3)
+                finish("dq", i - 1, 2, scopy)
+                group_b(i)
             grouped("a", i)
-            turn_a(i, 0, scopy)
-            turn_a(i, 1, scopy)
-            group_b(i)
-            if i == 0:
-                quantise("qk", 0, E4M3, 2 * D)
+            turn("a", i, 0)
+            turn("a", i, 1)
+            untangle("a", i, 0, scopy)
+            untangle("a", i, 1, scopy)
+            if i > 0:
+                finish("dq", i - 1, 3, scopy)
             if more:
                 quantise("v", n, E4M3)
-            if i > 0:
-                product("dq", i - 1, 2, scopy)
-                product("dq", i - 1, 3, scopy)
+                dp(n, 0)
+                dp(n, 1)
             quantise("b", i, E5M2)
+            product("dk", i, 0)
+            product("dk", i, 1)
             if more:
-                grouped("qk", n, 2 * D)
                 group_qk("k", n, 0, K_SHARE, scopy)
                 group_qk("q", n, 0, D, vcopy)
-                group_qk("k", n, K_SHARE, D, vcopy)
+            if i + 2 < B:
+                grouped("g", i + 2)
+                turn("g", i + 2, 0)
+                turn("g", i + 2, 1)
             quantise("a", i, E5M2)
+            finish("dk", i, 0, scopy)
+            finish("dk", i, 1, scopy if more else vcopy)
+            product("dk", i, 2)
+            product("dk", i, 3)
             if more:
+                group_qk("k", n, K_SHARE, D, vcopy)
                 quantise("qk", n, E4M3, 2 * D)
-            for t in range(4):
-                product("dk", i, t, scopy if more or t % 2 == 0 else vcopy)
-        for t in range(4):
-            product("dq", B - 1, t, scopy if t % 2 == 0 else vcopy, 1)
+            finish("dk", i, 2, scopy)
+            finish("dk", i, 3, scopy if more else vcopy)
+            product("dq", i, 0)
+            product("dq", i, 1)
+            if not more:
+                finish("dq", i, 0, scopy, 1)
+                finish("dq", i, 1, vcopy, 1)
+                product("dq", i, 2)
+                product("dq", i, 3)
+                finish("dq", i, 2, scopy, 1)
+                finish("dq", i, 3, vcopy, 1)

from contextlib import ExitStack

import concourse.mybir as mybir
from concourse.masks import make_identity

B, S, D = 8, 512, 512
FLOPS = 3 * 2 * B * S * S * D

F32 = mybir.dt.float32
BF16 = mybir.dt.bfloat16
U32 = mybir.dt.uint32
U8 = mybir.dt.uint8
E4M3 = mybir.dt.float8_e4m3fn_x4
E5M2 = mybir.dt.float8_e5m2_x4

P = 128
AHEAD = 3
K_SHARE = 320


def tile_retention_pa_v_kernel(tc, q_rot, k_rot, v, gamma, decay, grad_out, out_0, out_1):
    nc = tc.nc
    mult = mybir.AluOpType.mult

    with ExitStack() as ctx:
        const = ctx.enter_context(tc.tile_pool(name="const", bufs=1))
        loads = ctx.enter_context(tc.tile_pool(name="loads", bufs=AHEAD + 1))
        work = ctx.enter_context(tc.tile_pool(name="work", bufs=2))
        results = ctx.enter_context(tc.tile_pool(name="results", bufs=8))
        ps_tr = ctx.enter_context(tc.psum_pool(name="ps_tr", bufs=2))
        ps_dp = ctx.enter_context(tc.psum_pool(name="ps_dp", bufs=2))
        ps_out = ctx.enter_context(tc.psum_pool(name="ps_out", bufs=4))

        ident = const.tile([P, P], F32)
        make_identity(nc, ident[:])
        dec_nat = const.tile([P, 4, S], F32)
        dec = const.tile([P, 4, S], F32)

        ctx.enter_context(tc.manual_schedule())

        raw = {}
        grp = {}
        codes = {}
        dz = {}
        res = {}

        def rows4(x):
            return x.rearrange("(p j) d -> p j d", j=4)

        def load(name, x, b, pieces=1):
            t = loads.tile([P, 4, D], BF16, name="raw_" + name)
            w = 4 // pieces
            for h in range(pieces):
                nc.sync.dma_start(out=t[:, h * w : (h + 1) * w, :], in_=rows4(x[b])[:, h * w : (h + 1) * w, :])
            raw[name, b] = t

        def load_seq(b):
            load("g", grad_out, b)
            load("v", v, b)
            load("q", q_rot, b)
            load("k", k_rot, b)

        def grouped(name, b, width=S):
            t = work.tile([P, width, 4], BF16, name="grp_" + name, align_bytes=64)
            grp[name, b] = t

        def quantise(name, b, fmt, width=S):
            c = work.tile([P, width], U32, name="codes_" + name, align_bytes=64)
            s = work.tile([P, width], U8, name="scales_" + name, align_bytes=64)
            nc.vector.quantize_mx(
                out=c[:].bitcast(fmt), scales=s[:], in_=grp[name, b][:].rearrange("p w t -> p (w t)")
            )
            codes[name, b] = (c, s)

        banks = {}

        def turn(name, b, h):
            src = dz[b] if name == "a" else raw[name, b]
            words = src[:].bitcast(F32)
            ps = ps_tr.tile([P, 2, 2, P], F32, name="tr")
            for j in range(2):
                for u in range(2):
                    cols = slice(P * u, P * (u + 1)) if name == "a" else slice(u, 2 * P, 2)
                    nc.tensor.transpose(ps[:, j, u, :], words[:, 2 * h + j, cols], ident[:])
            banks[name, b, h] = ps

        def untangle(name, b, h, copy):
            ps = banks[name, b, h]
            order = "rj" if name == "v" else "jr"
            words = grp[name, b][:].rearrange("p w t -> p (w t)").bitcast(F32)[:, 512 * h : 512 * (h + 1)]
            if order == "jr":
                copy(out=words.rearrange("p (j r u) -> p j r u", j=2, u=2), in_=ps[:].rearrange("p j u r -> p j r u"))
            else:
                copy(out=words.rearrange("p (r j u) -> p r j u", j=2, u=2), in_=ps[:].rearrange("p j u r -> p r j u"))

        def mm(ps, lhs, rhs, j, rhs0=0):
            lc, ls = lhs
            rc, rs = rhs
            cols = slice(P * j, P * (j + 1))
            rcols = slice(rhs0, rhs0 + 512)
            nc.tensor.matmul_mx(
                out=ps[:],
                lhsT=lc[:, cols].bitcast(E5M2),
                lhsT_scale=ls[:, cols],
                rhs=rc[:, rcols].bitcast(E4M3),
                rhs_scale=rs[:, rcols],
                start=True,
                stop=True,
            )

        dps = {}

        def dp(b, t):
            ps = ps_dp.tile([P, S], F32, name="dp")
            mm(ps, codes["g", b], codes["v", b], t)
            dps[b, t] = ps

        def times_decay(b, t):
            if t == 0:
                dz_t = work.tile([P, 4, S], BF16, name="dz")
                dz[b] = dz_t
            nc.vector.tensor_tensor(out=dz[b][:, t, :], in0=dps[b, t][:], in1=dec[:, t, :], op=mult)

        def interleave(copy, dst, src):
            copy(out=dst.rearrange("p (c i) t -> p c t i", i=4), in_=src.rearrange("p t (c i) -> p c t i", i=4))

        def group_b(b):
            grouped("b", b)
            pairs = dz[b][:].rearrange("p t (u r e) -> p t u r e", u=2, e=2)
            for j in range(4):
                interleave(
                    nc.vector.tensor_copy, grp["b", b][:, P * j : P * (j + 1), :], pairs[:, :, j // 2, :, j % 2]
                )

        def group_qk(which, b, lo, hi, copy):
            o = 0 if which == "q" else D
            interleave(copy, grp["qk", b][:, o + lo : o + hi, :], raw[which, b][:, :, lo:hi])

        outs = {}

        def product(which, b, t):
            ps = ps_out.tile([P, D], F32, name="po")
            if which == "dq":
                mm(ps, codes["a", b], codes["qk", b], t, D)
            else:
                mm(ps, codes["b", b], codes["qk", b], t, 0)
            outs[which, b, t] = ps

        def finish(which, b, t, copy, per_store=2):
            dst = out_0 if which == "dq" else out_1
            if t % per_store == 0:
                r = results.tile([P, 2, D], F32, name="res")
                res[which] = r
            copy(out=res[which][:, t % per_store, :], in_=outs[which, b, t][:])
            if t % per_store == per_store - 1:
                t0 = t + 1 - per_store
                nc.sync.dma_start(out=rows4(dst[b])[:, t0 : t + 1, :], in_=res[which][:, 0:per_store, :])

        scopy = nc.scalar.copy
        vcopy = nc.vector.tensor_copy

        load("q", q_rot, 0)
        load("g", grad_out, 0, 2)
        load("k", k_rot, 0)
        load("v", v, 0, 2)
        for t in range(4):
            nc.sync.dma_start(out=dec_nat[:, t, :], in_=rows4(decay)[:, t, :])
        for b in range(1, AHEAD):
            load_seq(b)
        grouped("qk", 0, 2 * D)
        grouped("g", 0)
        grouped("v", 0)
        for w in range(4):
            ps = ps_out.tile([P, D], F32, name="po")
            nc.tensor.matmul(ps[:], lhsT=raw["q", 0][:, w % 4, 0:P], rhs=raw["q", 0][:, w % 4, :], start=True, stop=True)
        group_qk("q", 0, 0, 352, vcopy)
        group_qk("q", 0, 352, D, scopy)
        turn("g", 0, 0)
        turn("g", 0, 1)
        untangle("g", 0, 0, scopy)
        untangle("g", 0, 1, vcopy)
        group_qk("k", 0, 0, 384, vcopy)
        group_qk("k", 0, 384, D, scopy)
        for w in range(2):
            ps = ps_out.tile([P, D], F32, name="po")
            nc.tensor.matmul(ps[:], lhsT=raw["k", 0][:, w % 4, 0:P], rhs=raw["k", 0][:, w % 4, :], start=True, stop=True)
        quantise("g", 0, E5M2)
        turn("v", 0, 0)
        turn("v", 0, 1)
        untangle("v", 0, 0, scopy)
        untangle("v", 0, 1, scopy)
        for t in range(4):
            (vcopy if t < 1 else scopy)(
                out=dec[:, t, :].rearrange("p (u r e) -> p u r e", u=2, e=2),
                in_=dec_nat[:, t, :].rearrange("p (r u e) -> p u r e", u=2, e=2),
            )
            if t == 0:
                quantise("v", 0, E4M3)
                quantise("qk", 0, E4M3, 2 * D)
                dp(0, 0)
                dp(0, 1)

        for i in range(B):
            n = i + 1
            more = n < B
            if i + AHEAD < B:
                load_seq(i + AHEAD)
            if i == 0:
                grouped("g", n)
                turn("g", n, 0)
                turn("g", n, 1)
            times_decay(i, 0)
            times_decay(i, 1)
            dp(i, 2)
            dp(i, 3)
            times_decay(i, 2)
            times_decay(i, 3)
            if more:
                if i == 0:
                    group_b(0)
                untangle("g", n, 0, scopy)
                untangle("g", n, 1, scopy)
                quantise("g", n, E5M2)
            if i > 0:
                finish("dq", i - 1, 0, scopy)
                finish("dq", i - 1, 1, scopy)
            if more:
                grouped("v", n)
                grouped("qk", n, 2 * D)
                turn("v", n, 0)
                turn("v", n, 1)
                untangle("v", n, 0, scopy)
                untangle("v", n, 1, scopy)
            if i > 0:
                product("dq", i - 1, 2)
                product("dq", i - 1, 3)
                finish("dq", i - 1, 2, scopy)
                group_b(i)
            grouped("a", i)
            turn("a", i, 0)
            turn("a", i, 1)
            untangle("a", i, 0, scopy)
            untangle("a", i, 1, scopy)
            if i > 0:
                finish("dq", i - 1, 3, scopy)
            if more:
                quantise("v", n, E4M3)
                dp(n, 0)
                dp(n, 1)
            quantise("b", i, E5M2)
            product("dk", i, 0)
            product("dk", i, 1)
            if more:
                group_qk("k", n, 0, K_SHARE, scopy)
                group_qk("q", n, 0, D, vcopy)
            if i + 2 < B:
                grouped("g", i + 2)
                turn("g", i + 2, 0)
                turn("g", i + 2, 1)
            quantise("a", i, E5M2)
            finish("dk", i, 0, scopy)
            finish("dk", i, 1, scopy if more else vcopy)
            product("dk", i, 2)
            product("dk", i, 3)
            if more:
                group_qk("k", n, K_SHARE, D, vcopy)
                quantise("qk", n, E4M3, 2 * D)
            finish("dk", i, 2, scopy)
            finish("dk", i, 3, scopy if more else vcopy)
            product("dq", i, 0)
            product("dq", i, 1)
            if not more:
                finish("dq", i, 0, scopy, 1)
                finish("dq", i, 1, vcopy, 1)
                product("dq", i, 2)
                product("dq", i, 3)
                finish("dq", i, 2, scopy, 1)
                finish("dq", i, 3, vcopy, 1)
